import numpy as np
import ml_dtypes


def mxq(x, axis, fmt="e4m3"):
    dtype, down = {"e4m3": (ml_dtypes.float8_e4m3fn, 7), "e5m2": (ml_dtypes.float8_e5m2, 14)}[fmt]
    v = np.moveaxis(np.asarray(x, np.float32).astype(ml_dtypes.bfloat16).astype(np.float64), axis, -1)
    blocks = v.reshape(v.shape[:-1] + (-1, 32))
    amax = np.abs(blocks).max(-1, keepdims=True)
    byte = np.maximum(np.where(amax > 0, np.frexp(amax)[1] - 1 + 127, 0) - down, 1)
    scale = np.exp2(byte - 127.0)
    codes = (blocks / scale).astype(np.float32).astype(dtype).astype(np.float64)
    return np.moveaxis((codes * scale).reshape(v.shape), -1, axis)


WIDE = False


def mx_kscale(k):
    if not WIDE:
        return np.ones(k)
    levels = np.array([10, -10, 5, -5, 0])
    a = np.random.permutation(np.resize(levels, k // 512 * 4)).reshape(k // 512, 4)
    idx = np.arange(k)
    return np.exp2(a[idx // 512, idx % 128 // 32])


BF16 = ml_dtypes.bfloat16


def bf(x):
    return np.asarray(x, np.float32).astype(BF16)


def f64(x):
    return np.asarray(x).astype(np.float64)


E2M1 = np.array([0.0, 0.5, 1.0, 1.5, 2.0, 3.0, 4.0, 6.0, -0.0, -0.5, -1.0, -1.5, -2.0, -3.0, -4.0, -6.0])


def pack_weight(w, fmt):
    k, n = w.shape
    w = f64(bf(w)).reshape(k // 32, 32, n)
    amax = np.abs(w).max(1)
    if fmt == "e4m3":
        byte = np.frexp(amax)[1] - 1 + 127 - 7
    else:
        mant, ex = np.frexp(amax / 6.0)
        byte = np.where(mant > 0.5, ex, ex - 1) + 127
    byte = np.clip(np.where(amax > 0, byte, 1), 1, 254)
    scaled = (w * np.exp2(127.0 - byte)[:, None, :]).reshape(k, n).astype(np.float32)
    by_word = np.ascontiguousarray(scaled.reshape(k // 512, 128, 4, n).transpose(0, 1, 3, 2))
    if fmt == "e4m3":
        words = by_word.astype(ml_dtypes.float8_e4m3fn).view(np.uint8)
    else:
        c = by_word.astype(ml_dtypes.float4_e2m1fn).view(np.uint8) & 0xF
        words = c[..., 0::2] | (c[..., 1::2] << 4)
    return np.ascontiguousarray(words), np.ascontiguousarray(byte.astype(np.uint8).reshape(k // 512, 16, n))


def unpack_weight(words, scales, fmt):
    g, p, n, _ = words.shape
    if fmt == "e4m3":
        vals = np.ascontiguousarray(words).view(ml_dtypes.float8_e4m3fn).astype(np.float64)
    else:
        nib = np.empty((g, p, n, 4), np.uint8)
        nib[..., 0::2] = words & 0xF
        nib[..., 1::2] = words >> 4
        vals = E2M1[nib]
    vals = vals * np.repeat(np.exp2(scales.astype(np.float64) - 127.0), 8, axis=1)[..., None]
    return vals.transpose(0, 1, 3, 2).reshape(g * 512, n)

def pack4(w):
    words, scales = pack_weight(w, "e2m1")
    return words.reshape(words.shape[0], 128, -1), scales


def unpack4(words, scales):
    return unpack_weight(words.reshape(words.shape[0], 128, -1, 2), scales, "e2m1")


B, T, KA, KT, DIM, NH, HD, E = 2, 64, 256, 256, 16384, 8, 128, 8
ROPE_BASE = 10000.0


def rope_cos_sin(L, hd):
    inv_freq = 1.0 / (ROPE_BASE ** (f64(np.arange(0, hd, 2)) / hd))
    freqs = f64(np.arange(L))[:, None] * inv_freq[None, :]
    emb = np.concatenate([freqs, freqs], axis=-1)
    return np.cos(emb), np.sin(emb)


def rotate_half(x):
    x1 = x[..., 0::2]
    x2 = x[..., 1::2]
    return np.stack((-x2, x1), axis=-1).reshape(x.shape)


def rope(t, cos, sin):
    return t * cos[None, None] + rotate_half(t) * sin[None, None]


def heads(t):
    return t.reshape(B, -1, NH, HD).transpose(0, 2, 1, 3)


def setup_inputs():
    s = mx_kscale(DIM)
    c = 1.2 / np.sqrt(DIM)
    x = bf(np.random.standard_normal((B, T, DIM)) * s)
    qa_words, qa_scales = pack4((np.random.standard_normal((NH * HD, DIM)) * c / s[None, :]).T)
    b_qa = bf(np.random.standard_normal(NH * HD) * 0.3)
    qt_words, qt_scales = pack4((np.random.standard_normal((NH * HD, DIM)) * c / s[None, :]).T)
    b_qt = bf(np.random.standard_normal(NH * HD) * 0.3)
    return {"x": x,
            "W_qa_words": qa_words,
            "W_qa_scales": qa_scales,
            "b_qa": b_qa,
            "W_qt_words": qt_words,
            "W_qt_scales": qt_scales,
            "b_qt": b_qt}


def reference(x, W_qa_words, W_qa_scales, b_qa, W_qt_words, W_qt_scales, b_qt):
    xq = mxq(f64(x), 2, "e4m3")
    q_a = heads((xq @ unpack4(W_qa_words, W_qa_scales)) + f64(b_qa))
    q_t = heads((xq @ unpack4(W_qt_words, W_qt_scales)) + f64(b_qt))
    cos_m, sin_m = rope_cos_sin(T, HD)
    return rope(q_a, cos_m, sin_m), rope(q_t, cos_m, sin_m)

@@ -1,0 +1,262 @@
+import math
+from contextlib import ExitStack
+
+import concourse.mybir as mybir
+from concourse.masks import make_identity
+
+F32 = mybir.dt.float32
+BF16 = mybir.dt.bfloat16
+I32 = mybir.dt.int32
+U32 = mybir.dt.uint32
+U8 = mybir.dt.uint8
+FP8X4 = mybir.dt.float8_e4m3fn_x4
+FP4X4 = mybir.dt.float4_e2m1fn_x4
+ALU = mybir.AluOpType
+ACT = mybir.ActivationFunctionType
+
+P = 128
+SEQ = 64
+K = 16384
+K_PASS = 512
+PASSES = K // K_PASS
+FEATURES = 1024
+BANK = 512
+BANKS = FEATURES // BANK
+HEAD = 128
+HEADS_PER_BANK = BANK // HEAD
+ANGLES = 64
+ROPE_BASE = 10000.0
+
+X_LOAD_PASSES = 8
+QUANT_PASSES = 4
+W_LOAD_PASSES = 4
+W_BUFFERS = 8
+SCALE_LOAD_PASSES = 8
+
+ROUND_MAGIC = 12582912.0
+TWO_PI_HIGH = 6.28125
+TWO_PI_LOW = 2.0 * math.pi - TWO_PI_HIGH
+
+FLOPS = 2 * P * K * 2 * FEATURES
+
+
+def tile_l1regressionmoeactionhead_pa_k_kernel(
+    tc, x, W_qa_words, W_qa_scales, b_qa, W_qt_words, W_qt_scales, b_qt, out_0, out_1
+):
+    nc = tc.nc
+    with ExitStack() as ctx:
+        ctx.enter_context(tc.manual_schedule())
+        keep = ctx.enter_context(tc.tile_pool(name="keep", bufs=1))
+        x_pool = ctx.enter_context(tc.tile_pool(name="x_pool", bufs=K // (X_LOAD_PASSES * K_PASS)))
+        stage = ctx.enter_context(tc.tile_pool(name="stage", bufs=3))
+        w_pool = ctx.enter_context(tc.tile_pool(name="w_pool", bufs=W_BUFFERS))
+        work = ctx.enter_context(tc.tile_pool(name="work", bufs=2))
+        acc_pool = ctx.enter_context(tc.psum_pool(name="acc_pool", bufs=1))
+        bank_pool = ctx.enter_context(tc.psum_pool(name="bank_pool", bufs=4))
+
+        x_rows = x.flatten_outer_dims()
+        x_cols = X_LOAD_PASSES * K_PASS
+        x_tiles = []
+        for c in range(K // x_cols):
+            x_sb = x_pool.tile([P, x_cols], BF16, name="x_sb")
+            nc.sync.dma_start(out=x_sb[:], in_=x_rows[:, c * x_cols : (c + 1) * x_cols])
+            x_tiles.append(x_sb)
+
+        plane_a = keep.tile([P, PASSES, FEATURES], U8, align_bytes=64, name="plane_a")
+        plane_t = keep.tile([P, PASSES, FEATURES], U8, align_bytes=64, name="plane_t")
+        nc.vector.memset(plane_a[:].bitcast(I32), 0)
+
+        def load_scale_rows(plane, scales):
+            rows = scales.bitcast(I32).rearrange("g q w -> q g w")
+            for g0 in range(0, PASSES, SCALE_LOAD_PASSES):
+                g1 = g0 + SCALE_LOAD_PASSES
+                for q in range(8):
+                    first = 32 * (q // 4) + q % 4
+                    nc.sync.dma_start(
+                        out=plane[first:P:64, g0:g1, :].bitcast(I32),
+                        in_=rows[q:16:8, g0:g1, :],
+                    )
+
+        part_i = keep.tile([P, 1], I32, name="part_i")
+        nc.gpsimd.iota(part_i[:], pattern=[[0, 1]], base=0, channel_multiplier=1)
+        ident = keep.tile([P, P], F32, name="ident")
+        make_identity(nc, ident[:])
+        ones = keep.tile([P, P], BF16, name="ones")
+        nc.gpsimd.memset(ones[:], 1.0)
+        bias_rows = keep.tile([P, 2 * FEATURES], BF16, name="bias_rows")
+        nc.gpsimd.memset(bias_rows[:], 0.0)
+        nc.scalar.dma_start(out=bias_rows[0:1, 0:FEATURES], in_=b_qa.rearrange("(o n) -> o n", o=1))
+        nc.scalar.dma_start(
+            out=bias_rows[0:1, FEATURES : 2 * FEATURES], in_=b_qt.rearrange("(o n) -> o n", o=1)
+        )
+
+        pos_i = keep.tile([P, 1], I32, name="pos_i")
+        nc.vector.tensor_scalar(
+            out=pos_i[:], in0=part_i[:], scalar1=SEQ - 1, scalar2=None, op0=ALU.bitwise_and
+        )
+        pos = keep.tile([P, 1], F32, name="pos")
+        nc.vector.tensor_copy(out=pos[:], in_=pos_i[:])
+        ratio = ROPE_BASE ** (-1.0 / ANGLES)
+        half = ANGLES // 2
+        freq = keep.tile([P, 2, half], F32, name="freq")
+        nc.vector.memset(freq[:, 0, 0:1], 1.0)
+        for step in range(5):
+            width = 2**step
+            nc.vector.tensor_scalar(
+                out=freq[:, 0, width : 2 * width],
+                in0=freq[:, 0, 0:width],
+                scalar1=ratio ** (2 * width),
+                scalar2=None,
+                op0=ALU.mult,
+            )
+        nc.vector.tensor_scalar(
+            out=freq[:, 1, :], in0=freq[:, 0, :], scalar1=ratio, scalar2=None, op0=ALU.mult
+        )
+        freq_flat = freq[:].rearrange("p e i -> p (e i)")
+        angle = keep.tile([P, 2, ANGLES], F32, name="angle")
+        nc.vector.tensor_scalar(
+            out=angle[:, 0, :], in0=freq_flat, scalar1=pos[:, 0:1], scalar2=None, op0=ALU.mult
+        )
+        nc.vector.tensor_scalar(
+            out=angle[:, 1, :],
+            in0=freq_flat,
+            scalar1=pos[:, 0:1],
+            scalar2=0.5 * math.pi,
+            op0=ALU.mult,
+            op1=ALU.add,
+        )
+        angle_flat = angle[:].rearrange("p s j -> p (s j)")
+        turns = keep.tile([P, 2 * ANGLES], F32, name="turns")
+        nc.vector.tensor_scalar(
+            out=turns[:],
+            in0=angle_flat,
+            scalar1=0.5 / math.pi,
+            scalar2=ROUND_MAGIC,
+            op0=ALU.mult,
+            op1=ALU.add,
+        )
+        whole = keep.tile([P, 2 * ANGLES], F32, name="whole")
+        nc.vector.tensor_scalar(
+            out=whole[:], in0=turns[:], scalar1=ROUND_MAGIC, scalar2=None, op0=ALU.subtract
+        )
+        near = keep.tile([P, 2 * ANGLES], F32, name="near")
+        nc.vector.scalar_tensor_tensor(
+            out=near[:], in0=whole[:], scalar=-TWO_PI_HIGH, in1=angle_flat, op0=ALU.mult, op1=ALU.add
+        )
+        reduced = keep.tile([P, 2 * ANGLES], F32, name="reduced")
+        nc.vector.scalar_tensor_tensor(
+            out=reduced[:], in0=whole[:], scalar=-TWO_PI_LOW, in1=near[:], op0=ALU.mult, op1=ALU.add
+        )
+        trig = keep.tile([P, 4, half], F32, name="trig")
+        trig_flat = trig[:].rearrange("p s i -> p (s i)")
+        nc.scalar.activation(out=trig_flat[:, 0:half], in_=reduced[:, 0:half], func=ACT.Sin, scale=-1.0)
+        nc.scalar.activation(
+            out=trig_flat[:, half : 4 * half], in_=reduced[:, half : 4 * half], func=ACT.Sin
+        )
+        repeats = BANK // ANGLES
+        minus_sin_even = trig[:, 0, :].unsqueeze(1).to_broadcast([P, repeats, half])
+        sin_odd = trig[:, 1, :].unsqueeze(1).to_broadcast([P, repeats, half])
+        cos_both = trig[:, 2:4, :].unsqueeze(2).to_broadcast([P, 2, repeats, half])
+
+        x_codes = keep.tile([P, PASSES, P], U32, align_bytes=64, name="x_codes")
+        x_plane = keep.tile([P, PASSES, P], U8, align_bytes=64, name="x_plane")
+
+        def quantise(grouped, g0):
+            g1 = g0 + QUANT_PASSES
+            nc.vector.quantize_mx(
+                out=x_codes[:, g0:g1, :].rearrange("p g m -> p (g m)").bitcast(FP8X4),
+                scales=x_plane[:, g0:g1, :].rearrange("p g m -> p (g m)"),
+                in_=grouped[:],
+            )
+
+        waiting = None
+        for g0 in range(0, PASSES, QUANT_PASSES):
+            x_words = x_tiles[g0 // X_LOAD_PASSES][:].bitcast(F32)
+            grouped = stage.tile([P, QUANT_PASSES * K_PASS], BF16, align_bytes=64, name="grouped")
+            grouped_words = grouped[:].bitcast(F32).rearrange(
+                "p (g m u) -> p g m u", g=QUANT_PASSES, m=P, u=2
+            )
+            for pair in range(QUANT_PASSES // 2):
+                xt = bank_pool.tile([P, 2, 2, P], F32, name="xt", tag="bank")
+                for gl in range(2):
+                    first = (K_PASS // 2) * ((g0 + 2 * pair + gl) % X_LOAD_PASSES)
+                    for u in range(2):
+                        nc.tensor.transpose(
+                            xt[:, gl, u, :], x_words[:, first + u : first + K_PASS // 2 : 2], ident[:]
+                        )
+                copy_out = nc.vector.tensor_copy if pair % 2 == 0 else nc.scalar.copy
+                copy_out(
+                    out=grouped_words[:, 2 * pair : 2 * pair + 2],
+                    in_=xt[:].rearrange("p g u m -> p g m u"),
+                )
+            if waiting is not None:
+                quantise(waiting[0], waiting[1])
+            waiting = (grouped, g0)
+        quantise(waiting[0], waiting[1])
+        nc.vector.memset(plane_t[:].bitcast(I32), 0)
+
+        bias_split = keep.tile([P, 2 * BANKS, 2, BANK // 2], F32, name="bias_split")
+        for b in range(2 * BANKS):
+            bias_ps = bank_pool.tile([P, BANK], F32, name="bias_ps", tag="bank")
+            nc.tensor.matmul(
+                out=bias_ps[:], lhsT=ones[:], rhs=bias_rows[:, b * BANK : (b + 1) * BANK], start=True, stop=True
+            )
+            nc.scalar.copy(out=bias_split[:, b], in_=bias_ps[:].rearrange("p (c e) -> p e c", e=2))
+
+        def project(words, plane, accs):
+            for g0 in range(0, PASSES, W_LOAD_PASSES):
+                w_sb = w_pool.tile([P, W_LOAD_PASSES, 2 * FEATURES], U8, align_bytes=64, name="w_sb")
+                nc.sync.dma_start(
+                    out=w_sb[:].bitcast(I32),
+                    in_=words[g0 : g0 + W_LOAD_PASSES].bitcast(I32).rearrange("g p w -> p g w"),
+                )
+                for gl in range(W_LOAD_PASSES):
+                    g = g0 + gl
+                    for b in range(BANKS):
+                        nc.tensor.matmul_mx(
+                            out=accs[b][:],
+                            lhsT=x_codes[:, g, :].bitcast(FP8X4),
+                            lhsT_scale=x_plane[:, g, :],
+                            rhs=w_sb[:, gl, 2 * b * BANK : 2 * (b + 1) * BANK].bitcast(FP4X4),
+                            rhs_scale=plane[:, g, b * BANK : (b + 1) * BANK],
+                            start=(g == 0),
+                            stop=(g == PASSES - 1),
+                        )
+
+        def rotate_and_store(acc, bias, out, first_head, queue):
+            q = work.tile([P, 2, repeats, half], F32, name="q")
+            nc.vector.tensor_tensor(
+                out=q[:].rearrange("p e r i -> p e (r i)"),
+                in0=acc[:].rearrange("p (c e) -> p e c", e=2),
+                in1=bias,
+                op=ALU.add,
+            )
+            straight = work.tile([P, 2, repeats, half], F32, name="straight")
+            nc.vector.tensor_tensor(out=straight[:], in0=q[:], in1=cos_both, op=ALU.mult)
+            crossed = work.tile([P, 2, repeats, half], F32, name="crossed")
+            nc.vector.tensor_tensor(out=crossed[:, 0], in0=q[:, 1], in1=minus_sin_even, op=ALU.mult)
+            nc.vector.tensor_tensor(out=crossed[:, 1], in0=q[:, 0], in1=sin_odd, op=ALU.mult)
+            turned = work.tile([P, BANK], F32, name="turned")
+            nc.vector.tensor_tensor(
+                out=turned[:].rearrange("p (c e) -> p c e", e=2),
+                in0=straight[:].rearrange("p e r i -> p (r i) e"),
+                in1=crossed[:].rearrange("p e r i -> p (r i) e"),
+                op=ALU.add,
+            )
+            for n in range(P // SEQ):
+                queue.dma_start(
+                    out=out[n, first_head : first_head + HEADS_PER_BANK].rearrange("h t d -> t h d"),
+                    in_=turned[n * SEQ : (n + 1) * SEQ, :].rearrange("p (h d) -> p h d", d=HEAD),
+                )
+
+        acc_a = [acc_pool.tile([P, BANK], F32, name="acc_a%d" % b) for b in range(BANKS)]
+        acc_t = [acc_pool.tile([P, BANK], F32, name="acc_t%d" % b) for b in range(BANKS)]
+
+        load_scale_rows(plane_a, W_qa_scales)
+        project(W_qa_words, plane_a, acc_a)
+        load_scale_rows(plane_t, W_qt_scales)
+        for b in range(BANKS):
+            rotate_and_store(acc_a[b], bias_split[:, b], out_0, b * HEADS_PER_BANK, nc.scalar)
+        project(W_qt_words, plane_t, acc_t)
+        for b in range(BANKS):
+            rotate_and_store(acc_t[b], bias_split[:, BANKS + b], out_1, b * HEADS_PER_BANK, nc.sync)

@@ -31,7 +31,7 @@ X_LOAD_PASSES = 8
 QUANT_PASSES = 4
 W_LOAD_PASSES = 4
 W_BUFFERS = 8
-SCALE_LOAD_PASSES = 8
+SCALE_LOAD_PASSES = 32
 
 ROUND_MAGIC = 12582912.0
 TWO_PI_HIGH = 6.28125
@@ -67,13 +67,13 @@ def tile_l1regressionmoeactionhead_pa_k_kernel(
         nc.vector.memset(plane_a[:].bitcast(I32), 0)
 
         def load_scale_rows(plane, scales):
-            rows = scales.bitcast(I32).rearrange("g q w -> q g w")
+            rows = scales.bitcast(F32).rearrange("g q w -> q g w")
             for g0 in range(0, PASSES, SCALE_LOAD_PASSES):
                 g1 = g0 + SCALE_LOAD_PASSES
                 for q in range(8):
                     first = 32 * (q // 4) + q % 4
-                    nc.sync.dma_start(
-                        out=plane[first:P:64, g0:g1, :].bitcast(I32),
+                    nc.gpsimd.dma_start(
+                        out=plane[first:P:64, g0:g1, :].bitcast(F32),
                         in_=rows[q:16:8, g0:g1, :],
                     )
 

@@ -65,15 +65,16 @@ def tile_l1regressionmoeactionhead_pa_k_kernel(
         plane_a = keep.tile([P, PASSES, FEATURES], U8, align_bytes=64, name="plane_a")
         plane_t = keep.tile([P, PASSES, FEATURES], U8, align_bytes=64, name="plane_t")
         nc.vector.memset(plane_a[:].bitcast(I32), 0)
+        nc.vector.memset(plane_t[:].bitcast(I32), 0)
 
         def load_scale_rows(plane, scales):
-            rows = scales.bitcast(F32).rearrange("g q w -> q g w")
+            rows = scales.bitcast(I32).rearrange("g q w -> q g w")
             for g0 in range(0, PASSES, SCALE_LOAD_PASSES):
                 g1 = g0 + SCALE_LOAD_PASSES
                 for q in range(8):
                     first = 32 * (q // 4) + q % 4
-                    nc.gpsimd.dma_start(
-                        out=plane[first:P:64, g0:g1, :].bitcast(F32),
+                    nc.sync.dma_start(
+                        out=plane[first:P:64, g0:g1, :].bitcast(I32),
                         in_=rows[q:16:8, g0:g1, :],
                     )
 
@@ -193,7 +194,6 @@ def tile_l1regressionmoeactionhead_pa_k_kernel(
                 quantise(waiting[0], waiting[1])
             waiting = (grouped, g0)
         quantise(waiting[0], waiting[1])
-        nc.vector.memset(plane_t[:].bitcast(I32), 0)
 
         bias_split = keep.tile([P, 2 * BANKS, 2, BANK // 2], F32, name="bias_split")
         for b in range(2 * BANKS):
@@ -253,8 +253,8 @@ def tile_l1regressionmoeactionhead_pa_k_kernel(
         acc_t = [acc_pool.tile([P, BANK], F32, name="acc_t%d" % b) for b in range(BANKS)]
 
         load_scale_rows(plane_a, W_qa_scales)
-        project(W_qa_words, plane_a, acc_a)
         load_scale_rows(plane_t, W_qt_scales)
+        project(W_qa_words, plane_a, acc_a)
         for b in range(BANKS):
             rotate_and_store(acc_a[b], bias_split[:, b], out_0, b * HEADS_PER_BANK, nc.scalar)
         project(W_qt_words, plane_t, acc_t)

@@ -31,6 +31,8 @@ X_LOAD_PASSES = 8
 QUANT_PASSES = 4
 W_LOAD_PASSES = 4
 W_BUFFERS = 8
+END_FROM = 24
+END_LOAD_PASSES = 2
 SCALE_LOAD_PASSES = 32
 
 ROUND_MAGIC = 12582912.0
@@ -203,27 +205,29 @@ def tile_l1regressionmoeactionhead_pa_k_kernel(
             )
             nc.scalar.copy(out=bias_split[:, b], in_=bias_ps[:].rearrange("p (c e) -> p e c", e=2))
 
-        def project(words, plane, accs):
-            for g0 in range(0, PASSES, W_LOAD_PASSES):
-                w_sb = w_pool.tile([P, W_LOAD_PASSES, 2 * FEATURES], U8, align_bytes=64, name="w_sb")
-                nc.sync.dma_start(
-                    out=w_sb[:].bitcast(I32),
-                    in_=words[g0 : g0 + W_LOAD_PASSES].bitcast(I32).rearrange("g p w -> p g w"),
-                )
-                for gl in range(W_LOAD_PASSES):
-                    g = g0 + gl
-                    for b in range(BANKS):
-                        nc.tensor.matmul_mx(
-                            out=accs[b][:],
-                            lhsT=x_codes[:, g, :].bitcast(FP8X4),
-                            lhsT_scale=x_plane[:, g, :],
-                            rhs=w_sb[:, gl, 2 * b * BANK : 2 * (b + 1) * BANK].bitcast(FP4X4),
-                            rhs_scale=plane[:, g, b * BANK : (b + 1) * BANK],
-                            start=(g == 0),
-                            stop=(g == PASSES - 1),
-                        )
+        def load_and_multiply(words, plane, accs, g0, passes, b0, banks):
+            w_sb = w_pool.tile([P, passes, 2 * BANK * banks], U8, align_bytes=64, name="w_sb")
+            nc.sync.dma_start(
+                out=w_sb[:].bitcast(I32),
+                in_=words[g0 : g0 + passes, :, 2 * BANK * b0 : 2 * BANK * (b0 + banks)]
+                .bitcast(I32)
+                .rearrange("g p w -> p g w"),
+            )
+            for gl in range(passes):
+                g = g0 + gl
+                for bl in range(banks):
+                    b = b0 + bl
+                    nc.tensor.matmul_mx(
+                        out=accs[b][:],
+                        lhsT=x_codes[:, g, :].bitcast(FP8X4),
+                        lhsT_scale=x_plane[:, g, :],
+                        rhs=w_sb[:, gl, 2 * BANK * bl : 2 * BANK * (bl + 1)].bitcast(FP4X4),
+                        rhs_scale=plane[:, g, b * BANK : (b + 1) * BANK],
+                        start=(g == 0),
+                        stop=(g == PASSES - 1),
+                    )
 
-        def rotate_and_store(acc, bias, out, first_head, queue):
+        def rotate(acc, bias, turned):
             q = work.tile([P, 2, repeats, half], F32, name="q")
             nc.vector.tensor_tensor(
                 out=q[:].rearrange("p e r i -> p e (r i)"),
@@ -236,16 +240,18 @@ def tile_l1regressionmoeactionhead_pa_k_kernel(
             crossed = work.tile([P, 2, repeats, half], F32, name="crossed")
             nc.vector.tensor_tensor(out=crossed[:, 0], in0=q[:, 1], in1=minus_sin_even, op=ALU.mult)
             nc.vector.tensor_tensor(out=crossed[:, 1], in0=q[:, 0], in1=sin_odd, op=ALU.mult)
-            turned = work.tile([P, BANK], F32, name="turned")
             nc.vector.tensor_tensor(
                 out=turned[:].rearrange("p (c e) -> p c e", e=2),
                 in0=straight[:].rearrange("p e r i -> p (r i) e"),
                 in1=crossed[:].rearrange("p e r i -> p (r i) e"),
                 op=ALU.add,
             )
+
+        def store(turned, out, b):
+            heads = slice(b * HEADS_PER_BANK, (b + 1) * HEADS_PER_BANK)
             for n in range(P // SEQ):
-                queue.dma_start(
-                    out=out[n, first_head : first_head + HEADS_PER_BANK].rearrange("h t d -> t h d"),
+                nc.sync.dma_start(
+                    out=out[n, heads].rearrange("h t d -> t h d"),
                     in_=turned[n * SEQ : (n + 1) * SEQ, :].rearrange("p (h d) -> p h d", d=HEAD),
                 )
 
@@ -254,9 +260,19 @@ def tile_l1regressionmoeactionhead_pa_k_kernel(
 
         load_scale_rows(plane_a, W_qa_scales)
         load_scale_rows(plane_t, W_qt_scales)
-        project(W_qa_words, plane_a, acc_a)
+        turned_a = [keep.tile([P, BANK], F32, name="turned_a%d" % b) for b in range(BANKS)]
+        turned_t = [keep.tile([P, BANK], F32, name="turned_t%d" % b) for b in range(BANKS)]
+        for g0 in range(0, PASSES, W_LOAD_PASSES):
+            load_and_multiply(W_qa_words, plane_a, acc_a, g0, W_LOAD_PASSES, 0, BANKS)
         for b in range(BANKS):
-            rotate_and_store(acc_a[b], bias_split[:, b], out_0, b * HEADS_PER_BANK, nc.scalar)
-        project(W_qt_words, plane_t, acc_t)
+            rotate(acc_a[b], bias_split[:, b], turned_a[b])
+        for g0 in range(0, END_FROM, W_LOAD_PASSES):
+            load_and_multiply(W_qt_words, plane_t, acc_t, g0, W_LOAD_PASSES, 0, BANKS)
         for b in range(BANKS):
-            rotate_and_store(acc_t[b], bias_split[:, BANKS + b], out_1, b * HEADS_PER_BANK, nc.sync)
+            for g0 in range(END_FROM, PASSES, END_LOAD_PASSES):
+                load_and_multiply(W_qt_words, plane_t, acc_t, g0, END_LOAD_PASSES, b, 1)
+            rotate(acc_t[b], bias_split[:, BANKS + b], turned_t[b])
+        for b in range(BANKS):
+            store(turned_a[b], out_0, b)
+        for b in range(BANKS):
+            store(turned_t[b], out_1, b)

@@ -33,7 +33,7 @@ W_LOAD_PASSES = 4
 W_BUFFERS = 8
 END_FROM = 24
 END_LOAD_PASSES = 2
-SCALE_LOAD_PASSES = 32
+SCALE_ROW_PAIRS = 8
 
 ROUND_MAGIC = 12582912.0
 TWO_PI_HIGH = 6.28125
@@ -69,16 +69,10 @@ def tile_l1regressionmoeactionhead_pa_k_kernel(
         nc.vector.memset(plane_a[:].bitcast(I32), 0)
         nc.vector.memset(plane_t[:].bitcast(I32), 0)
 
-        def load_scale_rows(plane, scales):
+        def load_scale_row_pair(plane, scales, q):
             rows = scales.bitcast(I32).rearrange("g q w -> q g w")
-            for g0 in range(0, PASSES, SCALE_LOAD_PASSES):
-                g1 = g0 + SCALE_LOAD_PASSES
-                for q in range(8):
-                    first = 32 * (q // 4) + q % 4
-                    nc.sync.dma_start(
-                        out=plane[first:P:64, g0:g1, :].bitcast(I32),
-                        in_=rows[q:16:8, g0:g1, :],
-                    )
+            first = 32 * (q // 4) + q % 4
+            nc.sync.dma_start(out=plane[first:P:64].bitcast(I32), in_=rows[q:16:8])
 
         part_i = keep.tile([P, 1], I32, name="part_i")
         nc.gpsimd.iota(part_i[:], pattern=[[0, 1]], base=0, channel_multiplier=1)
@@ -258,12 +252,14 @@ def tile_l1regressionmoeactionhead_pa_k_kernel(
         acc_a = [acc_pool.tile([P, BANK], F32, name="acc_a%d" % b) for b in range(BANKS)]
         acc_t = [acc_pool.tile([P, BANK], F32, name="acc_t%d" % b) for b in range(BANKS)]
 
-        load_scale_rows(plane_a, W_qa_scales)
-        load_scale_rows(plane_t, W_qt_scales)
+        assert PASSES // W_LOAD_PASSES == SCALE_ROW_PAIRS
+        for q in range(SCALE_ROW_PAIRS):
+            load_scale_row_pair(plane_a, W_qa_scales, q)
         turned_a = [keep.tile([P, BANK], F32, name="turned_a%d" % b) for b in range(BANKS)]
         turned_t = [keep.tile([P, BANK], F32, name="turned_t%d" % b) for b in range(BANKS)]
         for g0 in range(0, PASSES, W_LOAD_PASSES):
             load_and_multiply(W_qa_words, plane_a, acc_a, g0, W_LOAD_PASSES, 0, BANKS)
+            load_scale_row_pair(plane_t, W_qt_scales, g0 // W_LOAD_PASSES)
         for b in range(BANKS):
             rotate(acc_a[b], bias_split[:, b], turned_a[b])
         for g0 in range(0, END_FROM, W_LOAD_PASSES):

@@ -34,6 +34,7 @@ W_BUFFERS = 8
 END_FROM = 24
 END_LOAD_PASSES = 2
 SCALE_ROW_PAIRS = 8
+RELEASE_PAIR = 4
 
 ROUND_MAGIC = 12582912.0
 TWO_PI_HIGH = 6.28125
@@ -69,10 +70,11 @@ def tile_l1regressionmoeactionhead_pa_k_kernel(
         nc.vector.memset(plane_a[:].bitcast(I32), 0)
         nc.vector.memset(plane_t[:].bitcast(I32), 0)
 
-        def load_scale_row_pair(plane, scales, q):
+        def load_scale_rows(plane, scales):
             rows = scales.bitcast(I32).rearrange("g q w -> q g w")
-            first = 32 * (q // 4) + q % 4
-            nc.sync.dma_start(out=plane[first:P:64].bitcast(I32), in_=rows[q:16:8])
+            for q in range(SCALE_ROW_PAIRS):
+                first = 32 * (q // 4) + q % 4
+                nc.sync.dma_start(out=plane[first:P:64].bitcast(I32), in_=rows[q:16:8])
 
         part_i = keep.tile([P, 1], I32, name="part_i")
         nc.gpsimd.iota(part_i[:], pattern=[[0, 1]], base=0, channel_multiplier=1)
@@ -199,8 +201,13 @@ def tile_l1regressionmoeactionhead_pa_k_kernel(
             )
             nc.scalar.copy(out=bias_split[:, b], in_=bias_ps[:].rearrange("p (c e) -> p e c", e=2))
 
-        def load_and_multiply(words, plane, accs, g0, passes, b0, banks):
+        def load_and_multiply(words, plane, accs, g0, passes, b0, banks, wait_for=None):
             w_sb = w_pool.tile([P, passes, 2 * BANK * banks], U8, align_bytes=64, name="w_sb")
+            if wait_for is not None:
+                row = 32 * (RELEASE_PAIR // 4)
+                nc.vector.tensor_copy(
+                    out=w_sb[row : row + 1, 0, 0:4].bitcast(I32), in_=wait_for[row : row + 1, 0, 0:4].bitcast(I32)
+                )
             nc.sync.dma_start(
                 out=w_sb[:].bitcast(I32),
                 in_=words[g0 : g0 + passes, :, 2 * BANK * b0 : 2 * BANK * (b0 + banks)]
@@ -252,14 +259,15 @@ def tile_l1regressionmoeactionhead_pa_k_kernel(
         acc_a = [acc_pool.tile([P, BANK], F32, name="acc_a%d" % b) for b in range(BANKS)]
         acc_t = [acc_pool.tile([P, BANK], F32, name="acc_t%d" % b) for b in range(BANKS)]
 
-        assert PASSES // W_LOAD_PASSES == SCALE_ROW_PAIRS
-        for q in range(SCALE_ROW_PAIRS):
-            load_scale_row_pair(plane_a, W_qa_scales, q)
+        load_scale_rows(plane_a, W_qa_scales)
+        load_scale_rows(plane_t, W_qt_scales)
         turned_a = [keep.tile([P, BANK], F32, name="turned_a%d" % b) for b in range(BANKS)]
         turned_t = [keep.tile([P, BANK], F32, name="turned_t%d" % b) for b in range(BANKS)]
+        assert RELEASE_PAIR % 4 == 0
         for g0 in range(0, PASSES, W_LOAD_PASSES):
-            load_and_multiply(W_qa_words, plane_a, acc_a, g0, W_LOAD_PASSES, 0, BANKS)
-            load_scale_row_pair(plane_t, W_qt_scales, g0 // W_LOAD_PASSES)
+            load_and_multiply(
+                W_qa_words, plane_a, acc_a, g0, W_LOAD_PASSES, 0, BANKS, wait_for=plane_t if g0 == 0 else None
+            )
         for b in range(BANKS):
             rotate(acc_a[b], bias_split[:, b], turned_a[b])
         for g0 in range(0, END_FROM, W_LOAD_PASSES):

@@ -34,7 +34,7 @@ W_BUFFERS = 8
 END_FROM = 24
 END_LOAD_PASSES = 2
 SCALE_ROW_PAIRS = 8
-RELEASE_PAIR = 4
+RELEASE_PAIR = 5
 
 ROUND_MAGIC = 12582912.0
 TWO_PI_HIGH = 6.28125
@@ -204,9 +204,9 @@ def tile_l1regressionmoeactionhead_pa_k_kernel(
         def load_and_multiply(words, plane, accs, g0, passes, b0, banks, wait_for=None):
             w_sb = w_pool.tile([P, passes, 2 * BANK * banks], U8, align_bytes=64, name="w_sb")
             if wait_for is not None:
-                row = 32 * (RELEASE_PAIR // 4)
+                rows = slice(32 * (RELEASE_PAIR // 4), 32 * (RELEASE_PAIR // 4) + RELEASE_PAIR % 4 + 1)
                 nc.vector.tensor_copy(
-                    out=w_sb[row : row + 1, 0, 0:4].bitcast(I32), in_=wait_for[row : row + 1, 0, 0:4].bitcast(I32)
+                    out=w_sb[rows, 0, 0:4].bitcast(I32), in_=wait_for[rows, 0, 0:4].bitcast(I32)
                 )
             nc.sync.dma_start(
                 out=w_sb[:].bitcast(I32),
@@ -263,7 +263,6 @@ def tile_l1regressionmoeactionhead_pa_k_kernel(
         load_scale_rows(plane_t, W_qt_scales)
         turned_a = [keep.tile([P, BANK], F32, name="turned_a%d" % b) for b in range(BANKS)]
         turned_t = [keep.tile([P, BANK], F32, name="turned_t%d" % b) for b in range(BANKS)]
-        assert RELEASE_PAIR % 4 == 0
         for g0 in range(0, PASSES, W_LOAD_PASSES):
             load_and_multiply(
                 W_qa_words, plane_a, acc_a, g0, W_LOAD_PASSES, 0, BANKS, wait_for=plane_t if g0 == 0 else None

@@ -24,6 +24,7 @@ BANK = 512
 BANKS = FEATURES // BANK
 HEAD = 128
 HEADS_PER_BANK = BANK // HEAD
+HALF = BANK // 2
 ANGLES = 64
 ROPE_BASE = 10000.0
 
@@ -96,29 +97,24 @@ def tile_l1regressionmoeactionhead_pa_k_kernel(
         pos = keep.tile([P, 1], F32, name="pos")
         nc.vector.tensor_copy(out=pos[:], in_=pos_i[:])
         ratio = ROPE_BASE ** (-1.0 / ANGLES)
-        half = ANGLES // 2
-        freq = keep.tile([P, 2, half], F32, name="freq")
-        nc.vector.memset(freq[:, 0, 0:1], 1.0)
-        for step in range(5):
+        freq = keep.tile([P, ANGLES], F32, name="freq")
+        nc.vector.memset(freq[:, 0:1], 1.0)
+        for step in range(6):
             width = 2**step
             nc.vector.tensor_scalar(
-                out=freq[:, 0, width : 2 * width],
-                in0=freq[:, 0, 0:width],
-                scalar1=ratio ** (2 * width),
+                out=freq[:, width : 2 * width],
+                in0=freq[:, 0:width],
+                scalar1=ratio**width,
                 scalar2=None,
                 op0=ALU.mult,
             )
-        nc.vector.tensor_scalar(
-            out=freq[:, 1, :], in0=freq[:, 0, :], scalar1=ratio, scalar2=None, op0=ALU.mult
-        )
-        freq_flat = freq[:].rearrange("p e i -> p (e i)")
         angle = keep.tile([P, 2, ANGLES], F32, name="angle")
         nc.vector.tensor_scalar(
-            out=angle[:, 0, :], in0=freq_flat, scalar1=pos[:, 0:1], scalar2=None, op0=ALU.mult
+            out=angle[:, 0, :], in0=freq[:], scalar1=pos[:, 0:1], scalar2=None, op0=ALU.mult
         )
         nc.vector.tensor_scalar(
             out=angle[:, 1, :],
-            in0=freq_flat,
+            in0=freq[:],
             scalar1=pos[:, 0:1],
             scalar2=0.5 * math.pi,
             op0=ALU.mult,
@@ -146,16 +142,21 @@ def tile_l1regressionmoeactionhead_pa_k_kernel(
         nc.vector.scalar_tensor_tensor(
             out=reduced[:], in0=whole[:], scalar=-TWO_PI_LOW, in1=near[:], op0=ALU.mult, op1=ALU.add
         )
-        trig = keep.tile([P, 4, half], F32, name="trig")
-        trig_flat = trig[:].rearrange("p s i -> p (s i)")
-        nc.scalar.activation(out=trig_flat[:, 0:half], in_=reduced[:, 0:half], func=ACT.Sin, scale=-1.0)
+        trig = keep.tile([P, 2, ANGLES], F32, name="trig")
+        trig_flat = trig[:].rearrange("p s j -> p (s j)")
+        nc.scalar.activation(out=trig[:, 0, 0:ANGLES:2], in_=reduced[:, 0:ANGLES:2], func=ACT.Sin, scale=-1.0)
+        nc.scalar.activation(out=trig[:, 0, 1:ANGLES:2], in_=reduced[:, 1:ANGLES:2], func=ACT.Sin)
         nc.scalar.activation(
-            out=trig_flat[:, half : 4 * half], in_=reduced[:, half : 4 * half], func=ACT.Sin
+            out=trig_flat[:, ANGLES : 2 * ANGLES], in_=reduced[:, ANGLES : 2 * ANGLES], func=ACT.Sin
         )
-        repeats = BANK // ANGLES
-        minus_sin_even = trig[:, 0, :].unsqueeze(1).to_broadcast([P, repeats, half])
-        sin_odd = trig[:, 1, :].unsqueeze(1).to_broadcast([P, repeats, half])
-        cos_both = trig[:, 2:4, :].unsqueeze(2).to_broadcast([P, 2, repeats, half])
+        repeats = HALF // ANGLES
+        sin_pairs = (
+            trig[:, 0, :]
+            .rearrange("p (i e) -> p i e", e=2)
+            .unsqueeze(1)
+            .to_broadcast([P, repeats, ANGLES // 2, 2])
+        )
+        cos_all = trig[:, 1, :].unsqueeze(1).to_broadcast([P, repeats, ANGLES])
 
         x_codes = keep.tile([P, PASSES, P], U32, align_bytes=64, name="x_codes")
         x_plane = keep.tile([P, PASSES, P], U8, align_bytes=64, name="x_plane")
@@ -193,13 +194,13 @@ def tile_l1regressionmoeactionhead_pa_k_kernel(
             waiting = (grouped, g0)
         quantise(waiting[0], waiting[1])
 
-        bias_split = keep.tile([P, 2 * BANKS, 2, BANK // 2], F32, name="bias_split")
+        bias_all = keep.tile([P, 2 * BANKS, BANK], F32, name="bias_all")
         for b in range(2 * BANKS):
             bias_ps = bank_pool.tile([P, BANK], F32, name="bias_ps", tag="bank")
             nc.tensor.matmul(
                 out=bias_ps[:], lhsT=ones[:], rhs=bias_rows[:, b * BANK : (b + 1) * BANK], start=True, stop=True
             )
-            nc.scalar.copy(out=bias_split[:, b], in_=bias_ps[:].rearrange("p (c e) -> p e c", e=2))
+            nc.scalar.copy(out=bias_all[:, b], in_=bias_ps[:])
 
         def load_and_multiply(words, plane, accs, g0, passes, b0, banks, wait_for=None):
             w_sb = w_pool.tile([P, passes, 2 * BANK * banks], U8, align_bytes=64, name="w_sb")
@@ -229,31 +230,36 @@ def tile_l1regressionmoeactionhead_pa_k_kernel(
                     )
 
         def rotate(acc, bias, turned):
-            q = work.tile([P, 2, repeats, half], F32, name="q")
-            nc.vector.tensor_tensor(
-                out=q[:].rearrange("p e r i -> p e (r i)"),
-                in0=acc[:].rearrange("p (c e) -> p e c", e=2),
-                in1=bias,
-                op=ALU.add,
-            )
-            straight = work.tile([P, 2, repeats, half], F32, name="straight")
-            nc.vector.tensor_tensor(out=straight[:], in0=q[:], in1=cos_both, op=ALU.mult)
-            crossed = work.tile([P, 2, repeats, half], F32, name="crossed")
-            nc.vector.tensor_tensor(out=crossed[:, 0], in0=q[:, 1], in1=minus_sin_even, op=ALU.mult)
-            nc.vector.tensor_tensor(out=crossed[:, 1], in0=q[:, 0], in1=sin_odd, op=ALU.mult)
-            nc.vector.tensor_tensor(
-                out=turned[:].rearrange("p (c e) -> p c e", e=2),
-                in0=straight[:].rearrange("p e r i -> p (r i) e"),
-                in1=crossed[:].rearrange("p e r i -> p (r i) e"),
-                op=ALU.add,
-            )
+            halves = [slice(0, HALF), slice(HALF, BANK)]
+            q = work.tile([P, BANK], F32, name="q")
+            straight = work.tile([P, BANK], F32, name="straight")
+            crossed = work.tile([P, BANK], F32, name="crossed")
+            for c in halves:
+                nc.vector.tensor_tensor(out=q[:, c], in0=acc[:, c], in1=bias[:, c], op=ALU.add)
+            for c in halves:
+                nc.vector.tensor_tensor(
+                    out=crossed[:, c].rearrange("p (r i e) -> p r i e", r=repeats, e=2),
+                    in0=q[:, c].rearrange("p (r i e) -> p r i e", r=repeats, e=2)[:, :, :, ::-1],
+                    in1=sin_pairs,
+                    op=ALU.mult,
+                )
+            for c in halves:
+                nc.vector.tensor_tensor(
+                    out=straight[:, c].rearrange("p (r j) -> p r j", r=repeats),
+                    in0=q[:, c].rearrange("p (r j) -> p r j", r=repeats),
+                    in1=cos_all,
+                    op=ALU.mult,
+                )
+            for c in halves:
+                nc.vector.tensor_tensor(out=turned[:, c], in0=straight[:, c], in1=crossed[:, c], op=ALU.add)
 
-        def store(turned, out, b):
-            heads = slice(b * HEADS_PER_BANK, (b + 1) * HEADS_PER_BANK)
-            for n in range(P // SEQ):
-                nc.sync.dma_start(
+        def store(turned, out, b, first, count):
+            heads = slice(b * HEADS_PER_BANK + first, b * HEADS_PER_BANK + first + count)
+            columns = slice(first * HEAD, (first + count) * HEAD)
+            for n, queue in ((0, nc.sync), (1, nc.scalar)):
+                queue.dma_start(
                     out=out[n, heads].rearrange("h t d -> t h d"),
-                    in_=turned[n * SEQ : (n + 1) * SEQ, :].rearrange("p (h d) -> p h d", d=HEAD),
+                    in_=turned[n * SEQ : (n + 1) * SEQ, columns].rearrange("p (h d) -> p h d", d=HEAD),
                 )
 
         acc_a = [acc_pool.tile([P, BANK], F32, name="acc_a%d" % b) for b in range(BANKS)]
@@ -268,14 +274,15 @@ def tile_l1regressionmoeactionhead_pa_k_kernel(
                 W_qa_words, plane_a, acc_a, g0, W_LOAD_PASSES, 0, BANKS, wait_for=plane_t if g0 == 0 else None
             )
         for b in range(BANKS):
-            rotate(acc_a[b], bias_split[:, b], turned_a[b])
+            rotate(acc_a[b], bias_all[:, b], turned_a[b])
         for g0 in range(0, END_FROM, W_LOAD_PASSES):
             load_and_multiply(W_qt_words, plane_t, acc_t, g0, W_LOAD_PASSES, 0, BANKS)
         for b in range(BANKS):
             for g0 in range(END_FROM, PASSES, END_LOAD_PASSES):
                 load_and_multiply(W_qt_words, plane_t, acc_t, g0, END_LOAD_PASSES, b, 1)
-            rotate(acc_t[b], bias_split[:, BANKS + b], turned_t[b])
+            rotate(acc_t[b], bias_all[:, BANKS + b], turned_t[b])
         for b in range(BANKS):
-            store(turned_a[b], out_0, b)
-        for b in range(BANKS):
-            store(turned_t[b], out_1, b)
+            store(turned_a[b], out_0, b, 0, HEADS_PER_BANK)
+        store(turned_t[0], out_1, 0, 0, HEADS_PER_BANK)
+        for first in range(0, HEADS_PER_BANK, HEADS_PER_BANK // 2):
+            store(turned_t[1], out_1, 1, first, HEADS_PER_BANK // 2)

@@ -31,7 +31,9 @@ ROPE_BASE = 10000.0
 X_LOAD_PASSES = 8
 QUANT_PASSES = 4
 W_LOAD_PASSES = 4
-W_BUFFERS = 8
+FIRST_LOADS = (1, 1, 2)
+WARM_UP = 6
+W_BUFFERS = 6
 END_FROM = 24
 END_LOAD_PASSES = 2
 SCALE_ROW_PAIRS = 8
@@ -54,6 +56,7 @@ def tile_l1regressionmoeactionhead_pa_k_kernel(
         x_pool = ctx.enter_context(tc.tile_pool(name="x_pool", bufs=K // (X_LOAD_PASSES * K_PASS)))
         stage = ctx.enter_context(tc.tile_pool(name="stage", bufs=3))
         w_pool = ctx.enter_context(tc.tile_pool(name="w_pool", bufs=W_BUFFERS))
+        end_pool = ctx.enter_context(tc.tile_pool(name="end_pool", bufs=2 * (PASSES - END_FROM) // END_LOAD_PASSES))
         work = ctx.enter_context(tc.tile_pool(name="work", bufs=2))
         acc_pool = ctx.enter_context(tc.psum_pool(name="acc_pool", bufs=1))
         bank_pool = ctx.enter_context(tc.psum_pool(name="bank_pool", bufs=4))
@@ -82,7 +85,6 @@ def tile_l1regressionmoeactionhead_pa_k_kernel(
         ident = keep.tile([P, P], F32, name="ident")
         make_identity(nc, ident[:])
         ones = keep.tile([P, P], BF16, name="ones")
-        nc.gpsimd.memset(ones[:], 1.0)
         bias_rows = keep.tile([P, 2 * FEATURES], BF16, name="bias_rows")
         nc.gpsimd.memset(bias_rows[:], 0.0)
         nc.scalar.dma_start(out=bias_rows[0:1, 0:FEATURES], in_=b_qa.rearrange("(o n) -> o n", o=1))
@@ -195,15 +197,21 @@ def tile_l1regressionmoeactionhead_pa_k_kernel(
         quantise(waiting[0], waiting[1])
 
         bias_all = keep.tile([P, 2 * BANKS, BANK], F32, name="bias_all")
-        for b in range(2 * BANKS):
-            bias_ps = bank_pool.tile([P, BANK], F32, name="bias_ps", tag="bank")
-            nc.tensor.matmul(
-                out=bias_ps[:], lhsT=ones[:], rhs=bias_rows[:, b * BANK : (b + 1) * BANK], start=True, stop=True
-            )
-            nc.scalar.copy(out=bias_all[:, b], in_=bias_ps[:])
 
-        def load_and_multiply(words, plane, accs, g0, passes, b0, banks, wait_for=None):
-            w_sb = w_pool.tile([P, passes, 2 * BANK * banks], U8, align_bytes=64, name="w_sb")
+        def spread_bias():
+            nc.vector.memset(ones[:], 1.0)
+            for b in range(2 * BANKS):
+                bias_ps = bank_pool.tile([P, BANK], F32, name="bias_ps", tag="bank")
+                nc.tensor.matmul(
+                    out=bias_ps[:], lhsT=ones[:], rhs=bias_rows[:, b * BANK : (b + 1) * BANK], start=True, stop=True
+                )
+                nc.scalar.copy(out=bias_all[:, b], in_=bias_ps[:])
+            for i in range(WARM_UP):
+                unused = bank_pool.tile([P, BANK], F32, name="unused", tag="bank")
+                nc.tensor.matmul(out=unused[:], lhsT=ones[:], rhs=bias_rows[:, 0:BANK], start=True, stop=True)
+
+        def load_and_multiply(words, plane, accs, g0, passes, b0, banks, wait_for=None, pool=w_pool, tag="w_sb"):
+            w_sb = pool.tile([P, passes, 2 * BANK * banks], U8, align_bytes=64, name="w_sb", tag=tag)
             if wait_for is not None:
                 rows = slice(32 * (RELEASE_PAIR // 4), 32 * (RELEASE_PAIR // 4) + RELEASE_PAIR % 4 + 1)
                 nc.vector.tensor_copy(
@@ -215,6 +223,8 @@ def tile_l1regressionmoeactionhead_pa_k_kernel(
                 .bitcast(I32)
                 .rearrange("g p w -> p g w"),
             )
+            if wait_for is not None:
+                spread_bias()
             for gl in range(passes):
                 g = g0 + gl
                 for bl in range(banks):
@@ -253,10 +263,10 @@ def tile_l1regressionmoeactionhead_pa_k_kernel(
             for c in halves:
                 nc.vector.tensor_tensor(out=turned[:, c], in0=straight[:, c], in1=crossed[:, c], op=ALU.add)
 
-        def store(turned, out, b, first, count):
+        def store(turned, out, b, first, count, queues=(nc.sync, nc.sync)):
             heads = slice(b * HEADS_PER_BANK + first, b * HEADS_PER_BANK + first + count)
             columns = slice(first * HEAD, (first + count) * HEAD)
-            for n, queue in ((0, nc.sync), (1, nc.scalar)):
+            for n, queue in enumerate(queues):
                 queue.dma_start(
                     out=out[n, heads].rearrange("h t d -> t h d"),
                     in_=turned[n * SEQ : (n + 1) * SEQ, columns].rearrange("p (h d) -> p h d", d=HEAD),
@@ -269,20 +279,22 @@ def tile_l1regressionmoeactionhead_pa_k_kernel(
         load_scale_rows(plane_t, W_qt_scales)
         turned_a = [keep.tile([P, BANK], F32, name="turned_a%d" % b) for b in range(BANKS)]
         turned_t = [keep.tile([P, BANK], F32, name="turned_t%d" % b) for b in range(BANKS)]
-        for g0 in range(0, PASSES, W_LOAD_PASSES):
+        g0 = 0
+        for passes in FIRST_LOADS + (W_LOAD_PASSES,) * ((PASSES - sum(FIRST_LOADS)) // W_LOAD_PASSES):
             load_and_multiply(
-                W_qa_words, plane_a, acc_a, g0, W_LOAD_PASSES, 0, BANKS, wait_for=plane_t if g0 == 0 else None
+                W_qa_words, plane_a, acc_a, g0, passes, 0, BANKS, wait_for=plane_t if g0 == 0 else None
             )
+            g0 += passes
         for b in range(BANKS):
             rotate(acc_a[b], bias_all[:, b], turned_a[b])
         for g0 in range(0, END_FROM, W_LOAD_PASSES):
             load_and_multiply(W_qt_words, plane_t, acc_t, g0, W_LOAD_PASSES, 0, BANKS)
         for b in range(BANKS):
             for g0 in range(END_FROM, PASSES, END_LOAD_PASSES):
-                load_and_multiply(W_qt_words, plane_t, acc_t, g0, END_LOAD_PASSES, b, 1)
+                load_and_multiply(W_qt_words, plane_t, acc_t, g0, END_LOAD_PASSES, b, 1, pool=end_pool, tag="end_sb")
             rotate(acc_t[b], bias_all[:, BANKS + b], turned_t[b])
         for b in range(BANKS):
             store(turned_a[b], out_0, b, 0, HEADS_PER_BANK)
         store(turned_t[0], out_1, 0, 0, HEADS_PER_BANK)
         for first in range(0, HEADS_PER_BANK, HEADS_PER_BANK // 2):
-            store(turned_t[1], out_1, 1, first, HEADS_PER_BANK // 2)
+            store(turned_t[1], out_1, 1, first, HEADS_PER_BANK // 2, queues=(nc.sync, nc.scalar))

import math
from contextlib import ExitStack

import concourse.mybir as mybir
from concourse.masks import make_identity

F32 = mybir.dt.float32
BF16 = mybir.dt.bfloat16
I32 = mybir.dt.int32
U32 = mybir.dt.uint32
U8 = mybir.dt.uint8
FP8X4 = mybir.dt.float8_e4m3fn_x4
FP4X4 = mybir.dt.float4_e2m1fn_x4
ALU = mybir.AluOpType
ACT = mybir.ActivationFunctionType

P = 128
SEQ = 64
K = 16384
K_PASS = 512
PASSES = K // K_PASS
FEATURES = 1024
BANK = 512
BANKS = FEATURES // BANK
HEAD = 128
HEADS_PER_BANK = BANK // HEAD
HALF = BANK // 2
ANGLES = 64
ROPE_BASE = 10000.0

X_LOAD_PASSES = 8
QUANT_PASSES = 4
W_LOAD_PASSES = 4
FIRST_LOADS = (1, 1, 2)
WARM_UP = 6
W_BUFFERS = 6
END_FROM = 24
END_LOAD_PASSES = 2
SCALE_ROW_PAIRS = 8
RELEASE_PAIR = 5

ROUND_MAGIC = 12582912.0
TWO_PI_HIGH = 6.28125
TWO_PI_LOW = 2.0 * math.pi - TWO_PI_HIGH

FLOPS = 2 * P * K * 2 * FEATURES


def tile_l1regressionmoeactionhead_pa_k_kernel(
    tc, x, W_qa_words, W_qa_scales, b_qa, W_qt_words, W_qt_scales, b_qt, out_0, out_1
):
    nc = tc.nc
    with ExitStack() as ctx:
        ctx.enter_context(tc.manual_schedule())
        keep = ctx.enter_context(tc.tile_pool(name="keep", bufs=1))
        x_pool = ctx.enter_context(tc.tile_pool(name="x_pool", bufs=K // (X_LOAD_PASSES * K_PASS)))
        stage = ctx.enter_context(tc.tile_pool(name="stage", bufs=3))
        w_pool = ctx.enter_context(tc.tile_pool(name="w_pool", bufs=W_BUFFERS))
        end_pool = ctx.enter_context(tc.tile_pool(name="end_pool", bufs=2 * (PASSES - END_FROM) // END_LOAD_PASSES))
        work = ctx.enter_context(tc.tile_pool(name="work", bufs=2))
        acc_pool = ctx.enter_context(tc.psum_pool(name="acc_pool", bufs=1))
        bank_pool = ctx.enter_context(tc.psum_pool(name="bank_pool", bufs=4))

        x_rows = x.flatten_outer_dims()
        x_cols = X_LOAD_PASSES * K_PASS
        x_tiles = []
        for c in range(K // x_cols):
            x_sb = x_pool.tile([P, x_cols], BF16, name="x_sb")
            nc.sync.dma_start(out=x_sb[:], in_=x_rows[:, c * x_cols : (c + 1) * x_cols])
            x_tiles.append(x_sb)

        plane_a = keep.tile([P, PASSES, FEATURES], U8, align_bytes=64, name="plane_a")
        plane_t = keep.tile([P, PASSES, FEATURES], U8, align_bytes=64, name="plane_t")
        nc.vector.memset(plane_a[:].bitcast(I32), 0)
        nc.vector.memset(plane_t[:].bitcast(I32), 0)

        def load_scale_rows(plane, scales):
            rows = scales.bitcast(I32).rearrange("g q w -> q g w")
            for q in range(SCALE_ROW_PAIRS):
                first = 32 * (q // 4) + q % 4
                nc.sync.dma_start(out=plane[first:P:64].bitcast(I32), in_=rows[q:16:8])

        part_i = keep.tile([P, 1], I32, name="part_i")
        nc.gpsimd.iota(part_i[:], pattern=[[0, 1]], base=0, channel_multiplier=1)
        ident = keep.tile([P, P], F32, name="ident")
        make_identity(nc, ident[:])
        ones = keep.tile([P, P], BF16, name="ones")
        bias_rows = keep.tile([P, 2 * FEATURES], BF16, name="bias_rows")
        nc.gpsimd.memset(bias_rows[:], 0.0)
        nc.scalar.dma_start(out=bias_rows[0:1, 0:FEATURES], in_=b_qa.rearrange("(o n) -> o n", o=1))
        nc.scalar.dma_start(
            out=bias_rows[0:1, FEATURES : 2 * FEATURES], in_=b_qt.rearrange("(o n) -> o n", o=1)
        )

        pos_i = keep.tile([P, 1], I32, name="pos_i")
        nc.vector.tensor_scalar(
            out=pos_i[:], in0=part_i[:], scalar1=SEQ - 1, scalar2=None, op0=ALU.bitwise_and
        )
        pos = keep.tile([P, 1], F32, name="pos")
        nc.vector.tensor_copy(out=pos[:], in_=pos_i[:])
        ratio = ROPE_BASE ** (-1.0 / ANGLES)
        freq = keep.tile([P, ANGLES], F32, name="freq")
        nc.vector.memset(freq[:, 0:1], 1.0)
        for step in range(6):
            width = 2**step
            nc.vector.tensor_scalar(
                out=freq[:, width : 2 * width],
                in0=freq[:, 0:width],
                scalar1=ratio**width,
                scalar2=None,
                op0=ALU.mult,
            )
        angle = keep.tile([P, 2, ANGLES], F32, name="angle")
        nc.vector.tensor_scalar(
            out=angle[:, 0, :], in0=freq[:], scalar1=pos[:, 0:1], scalar2=None, op0=ALU.mult
        )
        nc.vector.tensor_scalar(
            out=angle[:, 1, :],
            in0=freq[:],
            scalar1=pos[:, 0:1],
            scalar2=0.5 * math.pi,
            op0=ALU.mult,
            op1=ALU.add,
        )
        angle_flat = angle[:].rearrange("p s j -> p (s j)")
        turns = keep.tile([P, 2 * ANGLES], F32, name="turns")
        nc.vector.tensor_scalar(
            out=turns[:],
            in0=angle_flat,
            scalar1=0.5 / math.pi,
            scalar2=ROUND_MAGIC,
            op0=ALU.mult,
            op1=ALU.add,
        )
        whole = keep.tile([P, 2 * ANGLES], F32, name="whole")
        nc.vector.tensor_scalar(
            out=whole[:], in0=turns[:], scalar1=ROUND_MAGIC, scalar2=None, op0=ALU.subtract
        )
        near = keep.tile([P, 2 * ANGLES], F32, name="near")
        nc.vector.scalar_tensor_tensor(
            out=near[:], in0=whole[:], scalar=-TWO_PI_HIGH, in1=angle_flat, op0=ALU.mult, op1=ALU.add
        )
        reduced = keep.tile([P, 2 * ANGLES], F32, name="reduced")
        nc.vector.scalar_tensor_tensor(
            out=reduced[:], in0=whole[:], scalar=-TWO_PI_LOW, in1=near[:], op0=ALU.mult, op1=ALU.add
        )
        trig = keep.tile([P, 2, ANGLES], F32, name="trig")
        trig_flat = trig[:].rearrange("p s j -> p (s j)")
        nc.scalar.activation(out=trig[:, 0, 0:ANGLES:2], in_=reduced[:, 0:ANGLES:2], func=ACT.Sin, scale=-1.0)
        nc.scalar.activation(out=trig[:, 0, 1:ANGLES:2], in_=reduced[:, 1:ANGLES:2], func=ACT.Sin)
        nc.scalar.activation(
            out=trig_flat[:, ANGLES : 2 * ANGLES], in_=reduced[:, ANGLES : 2 * ANGLES], func=ACT.Sin
        )
        repeats = HALF // ANGLES
        sin_pairs = (
            trig[:, 0, :]
            .rearrange("p (i e) -> p i e", e=2)
            .unsqueeze(1)
            .to_broadcast([P, repeats, ANGLES // 2, 2])
        )
        cos_all = trig[:, 1, :].unsqueeze(1).to_broadcast([P, repeats, ANGLES])

        x_codes = keep.tile([P, PASSES, P], U32, align_bytes=64, name="x_codes")
        x_plane = keep.tile([P, PASSES, P], U8, align_bytes=64, name="x_plane")

        def quantise(grouped, g0):
            g1 = g0 + QUANT_PASSES
            nc.vector.quantize_mx(
                out=x_codes[:, g0:g1, :].rearrange("p g m -> p (g m)").bitcast(FP8X4),
                scales=x_plane[:, g0:g1, :].rearrange("p g m -> p (g m)"),
                in_=grouped[:],
            )

        waiting = None
        for g0 in range(0, PASSES, QUANT_PASSES):
            x_words = x_tiles[g0 // X_LOAD_PASSES][:].bitcast(F32)
            grouped = stage.tile([P, QUANT_PASSES * K_PASS], BF16, align_bytes=64, name="grouped")
            grouped_words = grouped[:].bitcast(F32).rearrange(
                "p (g m u) -> p g m u", g=QUANT_PASSES, m=P, u=2
            )
            for pair in range(QUANT_PASSES // 2):
                xt = bank_pool.tile([P, 2, 2, P], F32, name="xt", tag="bank")
                for gl in range(2):
                    first = (K_PASS // 2) * ((g0 + 2 * pair + gl) % X_LOAD_PASSES)
                    for u in range(2):
                        nc.tensor.transpose(
                            xt[:, gl, u, :], x_words[:, first + u : first + K_PASS // 2 : 2], ident[:]
                        )
                copy_out = nc.vector.tensor_copy if pair % 2 == 0 else nc.scalar.copy
                copy_out(
                    out=grouped_words[:, 2 * pair : 2 * pair + 2],
                    in_=xt[:].rearrange("p g u m -> p g m u"),
                )
            if waiting is not None:
                quantise(waiting[0], waiting[1])
            waiting = (grouped, g0)
        quantise(waiting[0], waiting[1])

        bias_all = keep.tile([P, 2 * BANKS, BANK], F32, name="bias_all")

        def spread_bias():
            nc.vector.memset(ones[:], 1.0)
            for b in range(2 * BANKS):
                bias_ps = bank_pool.tile([P, BANK], F32, name="bias_ps", tag="bank")
                nc.tensor.matmul(
                    out=bias_ps[:], lhsT=ones[:], rhs=bias_rows[:, b * BANK : (b + 1) * BANK], start=True, stop=True
                )
                nc.scalar.copy(out=bias_all[:, b], in_=bias_ps[:])
            for i in range(WARM_UP):
                unused = bank_pool.tile([P, BANK], F32, name="unused", tag="bank")
                nc.tensor.matmul(out=unused[:], lhsT=ones[:], rhs=bias_rows[:, 0:BANK], start=True, stop=True)

        def load_and_multiply(words, plane, accs, g0, passes, b0, banks, wait_for=None, pool=w_pool, tag="w_sb"):
            w_sb = pool.tile([P, passes, 2 * BANK * banks], U8, align_bytes=64, name="w_sb", tag=tag)
            if wait_for is not None:
                rows = slice(32 * (RELEASE_PAIR // 4), 32 * (RELEASE_PAIR // 4) + RELEASE_PAIR % 4 + 1)
                nc.vector.tensor_copy(
                    out=w_sb[rows, 0, 0:4].bitcast(I32), in_=wait_for[rows, 0, 0:4].bitcast(I32)
                )
            nc.sync.dma_start(
                out=w_sb[:].bitcast(I32),
                in_=words[g0 : g0 + passes, :, 2 * BANK * b0 : 2 * BANK * (b0 + banks)]
                .bitcast(I32)
                .rearrange("g p w -> p g w"),
            )
            if wait_for is not None:
                spread_bias()
            for gl in range(passes):
                g = g0 + gl
                for bl in range(banks):
                    b = b0 + bl
                    nc.tensor.matmul_mx(
                        out=accs[b][:],
                        lhsT=x_codes[:, g, :].bitcast(FP8X4),
                        lhsT_scale=x_plane[:, g, :],
                        rhs=w_sb[:, gl, 2 * BANK * bl : 2 * BANK * (bl + 1)].bitcast(FP4X4),
                        rhs_scale=plane[:, g, b * BANK : (b + 1) * BANK],
                        start=(g == 0),
                        stop=(g == PASSES - 1),
                    )

        def rotate(acc, bias, turned):
            halves = [slice(0, HALF), slice(HALF, BANK)]
            q = work.tile([P, BANK], F32, name="q")
            straight = work.tile([P, BANK], F32, name="straight")
            crossed = work.tile([P, BANK], F32, name="crossed")
            for c in halves:
                nc.vector.tensor_tensor(out=q[:, c], in0=acc[:, c], in1=bias[:, c], op=ALU.add)
            for c in halves:
                nc.vector.tensor_tensor(
                    out=crossed[:, c].rearrange("p (r i e) -> p r i e", r=repeats, e=2),
                    in0=q[:, c].rearrange("p (r i e) -> p r i e", r=repeats, e=2)[:, :, :, ::-1],
                    in1=sin_pairs,
                    op=ALU.mult,
                )
            for c in halves:
                nc.vector.tensor_tensor(
                    out=straight[:, c].rearrange("p (r j) -> p r j", r=repeats),
                    in0=q[:, c].rearrange("p (r j) -> p r j", r=repeats),
                    in1=cos_all,
                    op=ALU.mult,
                )
            for c in halves:
                nc.vector.tensor_tensor(out=turned[:, c], in0=straight[:, c], in1=crossed[:, c], op=ALU.add)

        def store(turned, out, b, first, count, queues=(nc.sync, nc.sync)):
            heads = slice(b * HEADS_PER_BANK + first, b * HEADS_PER_BANK + first + count)
            columns = slice(first * HEAD, (first + count) * HEAD)
            for n, queue in enumerate(queues):
                queue.dma_start(
                    out=out[n, heads].rearrange("h t d -> t h d"),
                    in_=turned[n * SEQ : (n + 1) * SEQ, columns].rearrange("p (h d) -> p h d", d=HEAD),
                )

        acc_a = [acc_pool.tile([P, BANK], F32, name="acc_a%d" % b) for b in range(BANKS)]
        acc_t = [acc_pool.tile([P, BANK], F32, name="acc_t%d" % b) for b in range(BANKS)]

        load_scale_rows(plane_a, W_qa_scales)
        load_scale_rows(plane_t, W_qt_scales)
        turned_a = [keep.tile([P, BANK], F32, name="turned_a%d" % b) for b in range(BANKS)]
        turned_t = [keep.tile([P, BANK], F32, name="turned_t%d" % b) for b in range(BANKS)]
        g0 = 0
        for passes in FIRST_LOADS + (W_LOAD_PASSES,) * ((PASSES - sum(FIRST_LOADS)) // W_LOAD_PASSES):
            load_and_multiply(
                W_qa_words, plane_a, acc_a, g0, passes, 0, BANKS, wait_for=plane_t if g0 == 0 else None
            )
            g0 += passes
        for b in range(BANKS):
            rotate(acc_a[b], bias_all[:, b], turned_a[b])
        for g0 in range(0, END_FROM, W_LOAD_PASSES):
            load_and_multiply(W_qt_words, plane_t, acc_t, g0, W_LOAD_PASSES, 0, BANKS)
        for b in range(BANKS):
            for g0 in range(END_FROM, PASSES, END_LOAD_PASSES):
                load_and_multiply(W_qt_words, plane_t, acc_t, g0, END_LOAD_PASSES, b, 1, pool=end_pool, tag="end_sb")
            rotate(acc_t[b], bias_all[:, BANKS + b], turned_t[b])
        for b in range(BANKS):
            store(turned_a[b], out_0, b, 0, HEADS_PER_BANK)
        store(turned_t[0], out_1, 0, 0, HEADS_PER_BANK)
        for first in range(0, HEADS_PER_BANK, HEADS_PER_BANK // 2):
            store(turned_t[1], out_1, 1, first, HEADS_PER_BANK // 2, queues=(nc.sync, nc.scalar))
